import numpy as np
import ml_dtypes


def mxq(x, axis, fmt="e4m3"):
    dtype, down = {"e4m3": (ml_dtypes.float8_e4m3fn, 7), "e5m2": (ml_dtypes.float8_e5m2, 14)}[fmt]
    v = np.moveaxis(np.asarray(x, np.float32).astype(ml_dtypes.bfloat16).astype(np.float64), axis, -1)
    blocks = v.reshape(v.shape[:-1] + (-1, 32))
    amax = np.abs(blocks).max(-1, keepdims=True)
    byte = np.maximum(np.where(amax > 0, np.frexp(amax)[1] - 1 + 127, 0) - down, 1)
    scale = np.exp2(byte - 127.0)
    codes = (blocks / scale).astype(np.float32).astype(dtype).astype(np.float64)
    return np.moveaxis((codes * scale).reshape(v.shape), -1, axis)


WIDE = False


def mx_kscale(k):
    if not WIDE:
        return np.ones(k)
    levels = np.array([18, -18])
    if k % 512:
        return np.exp2(np.random.permutation(np.resize(levels, k // 32))).repeat(32)
    a = np.empty((k // 512, 16))
    for p in range(k // 512):
        a[p, :8] = np.random.permutation(np.resize(levels, 8))
        for g in range(8):
            far = levels[np.abs(levels - a[p, g]) >= 10]
            a[p, g + 8] = far[np.random.randint(len(far))]
    return np.exp2(a.ravel()).repeat(32)


BF16 = ml_dtypes.bfloat16


def bf(x):
    return np.asarray(x, np.float32).astype(BF16)


def f64(x):
    return np.asarray(x).astype(np.float64)


B, D = 1536, 1024


def softplus(v):
    return np.logaddexp(v, 0.0)


def sigmoid(v):
    return 1.0 / (1.0 + np.exp(-v))


def setup_inputs():
    s = mx_kscale(B)[:, None]
    u = mx_kscale(D)
    xt0 = bf(np.random.standard_normal((B, D)) * 1.3)
    eps = bf(np.random.standard_normal((B, D)))
    x = bf(np.random.standard_normal((B, D)))
    t_rand = bf(np.random.uniform(0.0, 1.0, (B, 1)))
    Wm0 = bf(np.random.standard_normal((D, D)) / np.sqrt(D))
    bm = bf(np.random.standard_normal(D) * 0.5)
    Wv0 = bf(np.random.standard_normal((D, D)) / np.sqrt(D))
    bv = bf(np.random.standard_normal(D) * 0.5)
    g = bf(4.0 * np.random.standard_normal((B, D)) * np.exp2(np.random.randint(-6, 1, (B, 1))) / s * u)
    v = f64(xt0) @ f64(Wv0).T + f64(bv)
    return {"xt": bf(f64(xt0) * s), "eps": eps, "x": x, "t_rand": t_rand,
            "Wm": bf(f64(Wm0) / u[:, None]), "bm": bm,
            "Wv": bf(f64(Wv0) / u[:, None]), "bv": bv,
            "v": np.asarray(v, np.float32), "grad_out": g}


def reference(xt, eps, x, t_rand, Wm, bm, Wv, bv, v, grad_out):
    dmu = f64(t_rand) * f64(grad_out)
    dv = dmu * f64(eps) * sigmoid(f64(v))
    dz = np.concatenate([dmu, dv], 1)
    w = np.concatenate([f64(Wm), f64(Wv)], 0)
    dxt = mxq(dz, 1, "e5m2") @ mxq(w, 0, "e4m3")
    dWv = mxq(dv, 0, "e5m2").T @ mxq(f64(xt), 0, "e4m3")
    return dxt, dWv

@@ -1,0 +1,296 @@
+from contextlib import ExitStack
+
+import concourse.mybir as mybir
+from concourse.masks import make_identity
+
+B, D = 1536, 1024
+P = 128
+PACK = 4
+GROUPS = B // (P * PACK)
+N_TILE = 512
+LOADS = "g0/0/2 w0/0/4 e0/0/2 v0/0/2 w2/0/4 g0/2/4 w1/0/4 w3/0/4 e0/2/4 v0/2/4 g1/0/4 v1/2/4 v1/0/2 e1/0/4"
+GRP = 4
+M_LAG = 3
+EV = "SVSVVSSVVSVSVSVSSSSVSVSS"
+TAIL = {(0, 0), (0, 4), (1, 0)}
+BG = {0:"wi00V wi01S wq00 wi20V wq01",1:"wi21S wi11S wq21 wi31S wq20",2:"wi30V wi10S wq31 wq30 wq11",3:"wq10",5:"di00S",7:"di01S",8:"di10S dq01 dq00",11:"di11S dq10",12:"di20V di21S xi00V dq21 dq20 xq00 dq11",13:"xi10V",14:"xq10 xi20S",15:"xi11S xi21V xi01V xq20 xq21",99:"xq11 xq01"}
+FLOPS = 2 * B * D * D * 3
+BYTES = 2 * (3 * B * D + 2 * D * D + B) + 4 * B * D + 4 * (B * D + D * D)
+
+F32 = mybir.dt.float32
+BF16 = mybir.dt.bfloat16
+U32 = mybir.dt.uint32
+U8 = mybir.dt.uint8
+E4M3 = mybir.dt.float8_e4m3fn_x4
+E5M2 = mybir.dt.float8_e5m2_x4
+MULT = mybir.AluOpType.mult
+SIGMOID = mybir.ActivationFunctionType.Sigmoid
+
+
+def tile_diffscm_pb_v_kernel(
+    tc, xt, eps, x, t_rand, Wm, bm, Wv, bv, v, grad_out, out_0, out_1
+):
+    nc = tc.nc
+    by_group = lambda a: a.rearrange("(g p j) w -> p g j w", g=GROUPS, j=PACK)
+    xt_v, eps_v, v_v, grad_v, out0_v = [by_group(a) for a in (xt, eps, v, grad_out, out_0)]
+    w_v = [w.rearrange("(g p j) w -> p g j w", g=2, j=PACK) for w in (Wm, Wv)]
+
+    with ExitStack() as ctx:
+        const = ctx.enter_context(tc.tile_pool(name="const", bufs=1))
+        inp = ctx.enter_context(tc.tile_pool(name="inp", bufs=1))
+        keep = ctx.enter_context(tc.tile_pool(name="keep", bufs=1))
+        work = ctx.enter_context(tc.tile_pool(name="work", bufs=1))
+        psum = ctx.enter_context(tc.psum_pool(name="psum", bufs=4))
+        ctx.enter_context(tc.manual_schedule())
+
+        t_bf = const.tile([P, GROUPS, PACK], BF16, name="t_bf")
+        t_f = const.tile([P, GROUPS, PACK], F32, name="t_f")
+        warm = const.tile([P, 1], F32, name="warm")
+        ident = const.tile([P, P], F32, name="ident")
+
+        w_codes = keep.tile([P, 4, D], U32, align_bytes=64, name="w_codes")
+        w_scales = keep.tile([P, 4, D], U8, align_bytes=64, name="w_scales")
+        x_codes = keep.tile([P, GROUPS, D], U32, align_bytes=64, name="x_codes")
+        x_scales = keep.tile([P, GROUPS, D], U8, align_bytes=64, name="x_scales")
+        d_codes = keep.tile([P, GROUPS, D], U32, align_bytes=64, name="d_codes")
+        d_scales = keep.tile([P, GROUPS, D], U8, align_bytes=64, name="d_scales")
+
+        raw = {}
+
+        def load(key, view):
+            tile = inp.tile([P, PACK, D], BF16, tag="bf", bufs=8, name="raw_bf")
+            raw[key] = (tile, view)
+
+        def fetch(key, lo=0, hi=PACK):
+            tile, view = raw[key]
+            nc.sync.dma_start(out=tile[:, lo:hi, :], in_=view[:, lo:hi, :])
+
+        def load_v(g):
+            tile = inp.tile([P, PACK, D], F32, tag="v", bufs=2, name="raw_v")
+            raw["v", g] = (tile, v_v[:, g])
+
+        def load_group(g):
+            load(("g", g), grad_v[:, g])
+            load(("e", g), eps_v[:, g])
+            load_v(g)
+
+        for i in range(4):
+            load(("w", i), w_v[i // 2][:, i % 2])
+        load_group(0)
+        load_group(1)
+        nc.scalar.dma_start(out=t_bf[:], in_=t_rand.rearrange("(g p j) o -> p g (j o)", g=GROUPS, j=PACK))
+        for item in LOADS.split():
+            key, lo, hi = item.split("/")
+            fetch((key[0], int(key[1])), int(lo), int(hi))
+
+        nc.gpsimd.memset(warm[:], 0.0)
+        nc.scalar.activation(out=warm[:], in_=warm[:], func=SIGMOID)
+        make_identity(nc, ident[:])
+        nc.vector.tensor_copy(out=t_f[:], in_=t_bf[:])
+
+        def interleave(engine, src, half):
+            grp = work.tile([P, N_TILE, PACK], BF16, tag="grp", bufs=GRP, align_bytes=64, name="grp")
+            cols = src[:, :, half * N_TILE : (half + 1) * N_TILE]
+            dst_ap = grp[:].rearrange("p (c i) t -> p c t i", i=4)
+            src_ap = cols.rearrange("p t (c i) -> p c t i", i=4)
+            if engine == "V":
+                nc.vector.tensor_copy(out=dst_ap, in_=src_ap)
+            else:
+                nc.scalar.copy(out=dst_ap, in_=src_ap)
+            return grp
+
+        def quantize(grp, codes, scales, fmt):
+            nc.vector.quantize_mx(
+                out=codes.bitcast(fmt), scales=scales, in_=grp[:].rearrange("p c t -> p (c t)")
+            )
+
+        pending = {}
+
+        def w_inter(i, h, engine):
+            pending["w", i, h] = interleave(engine, raw["w", i][0], h)
+
+        def w_quant(i, h):
+            c = slice(h * N_TILE, (h + 1) * N_TILE)
+            quantize(pending["w", i, h], w_codes[:, i, c], w_scales[:, i, c], E4M3)
+
+        def x_inter(g, h, engine):
+            pending["x", g, h] = interleave(engine, raw["x", g][0], h)
+
+        def x_quant(g, h):
+            c = slice(h * N_TILE, (h + 1) * N_TILE)
+            quantize(pending["x", g, h], x_codes[:, g, c], x_scales[:, g, c], E4M3)
+
+        dv = {}
+
+        def d_inter(g, h, engine):
+            pending["d", g, h] = interleave(engine, dv[g], h)
+
+        def d_quant(g, h):
+            c = slice(h * N_TILE, (h + 1) * N_TILE)
+            quantize(pending["d", g, h], d_codes[:, g, c], d_scales[:, g, c], E5M2)
+
+        dmu, u, dzt, tps, dz = {}, {}, {}, {}, {}
+
+        def front(s):
+            g, j = divmod(s, PACK)
+            grad = raw["g", g][0][:, j, :]
+            dmu[s] = work.tile([P, D], BF16, tag="dmu", bufs=4, name="dmu")
+            nc.vector.tensor_scalar(out=dmu[s][:], in0=grad, scalar1=t_f[:, g, j : j + 1], scalar2=None, op0=MULT)
+
+        def product(s):
+            g, j = divmod(s, PACK)
+            u[s] = work.tile([P, D], F32, tag="u", bufs=2, name="u")
+            nc.vector.scalar_tensor_tensor(
+                out=u[s][:], in0=raw["g", g][0][:, j, :], scalar=t_f[:, g, j : j + 1],
+                in1=raw["e", g][0][:, j, :], op0=MULT, op1=MULT,
+            )
+
+        def sig(s):
+            g, j = divmod(s, PACK)
+            vv = raw["v", g][0][:, j, :]
+            nc.scalar.activation(out=vv, in_=vv, func=SIGMOID)
+
+        def spread(s):
+            g, j = divmod(s, PACK)
+            if j == 0:
+                dv[g] = work.tile([P, PACK, D], BF16, tag="dv", bufs=2, name="dv")
+            nc.vector.tensor_tensor(out=dv[g][:, j, :], in0=u[s][:], in1=raw["v", g][0][:, j, :], op=MULT)
+
+        def turn(s):
+            g, j = divmod(s, PACK)
+            for head, src in ((0, dmu[s][:]), (1, dv[g][:, j, :])):
+                words = src.bitcast(F32)
+                tp = psum.tile([P, 2, 2, P], F32, tag="tp", bufs=4, name="tp")
+                for k in range(2):
+                    for w in range(2):
+                        nc.tensor.transpose(tp[:, k, w, :], words[:, 256 * k + w : 256 * (k + 1) : 2], ident[:])
+                tps[s, head] = tp
+
+        def turn_out(s):
+            dzt[s] = work.tile([P, 2, 2, P, PACK], BF16, tag="dzt", bufs=3, align_bytes=64, name="dzt")
+            for head in range(2):
+                dst = dzt[s][:, head].rearrange("p k c t -> p (k c t)").bitcast(F32)
+                nc.scalar.copy(
+                    out=dst.rearrange("p (k c w) -> p k c w", k=2, w=2),
+                    in_=tps[s, head][:].rearrange("p k w c -> p k c w"),
+                )
+
+        def z_quant(s):
+            codes = work.tile([P, 4 * P], U32, tag="zc", bufs=4, align_bytes=64, name="zc")
+            scales = work.tile([P, 4 * P], U8, tag="zs", bufs=4, align_bytes=64, name="zs")
+            nc.vector.quantize_mx(
+                out=codes[:].bitcast(E5M2), scales=scales[:],
+                in_=dzt[s][:].rearrange("p h k c t -> p (h k c t)"),
+            )
+            dz[s] = (codes, scales)
+
+        acc = {}
+
+        def m_pass(s):
+            codes, scales = dz[s]
+            for n in range(2):
+                acc[s, n] = psum.tile([P, N_TILE], F32, tag="acc", bufs=4, name="acc")
+                cols = slice(n * N_TILE, (n + 1) * N_TILE)
+                for i in range(4):
+                    rows = slice(i * P, (i + 1) * P)
+                    nc.tensor.matmul_mx(
+                        out=acc[s, n][:],
+                        lhsT=codes[:, rows].bitcast(E5M2), lhsT_scale=scales[:, rows],
+                        rhs=w_codes[:, i, cols].bitcast(E4M3), rhs_scale=w_scales[:, i, cols],
+                        start=(i == 0), stop=(i == 3),
+                    )
+
+        def m_out(s, engines):
+            g, j = divmod(s, PACK)
+            res = work.tile([P, D], F32, tag="res", bufs=4, name="res")
+            for n in range(2):
+                dst = res[:, n * N_TILE : (n + 1) * N_TILE]
+                if engines[n] == "V":
+                    nc.vector.tensor_copy(out=dst, in_=acc[s, n][:])
+                else:
+                    nc.scalar.copy(out=dst, in_=acc[s, n][:])
+            nc.sync.dma_start(out=out0_v[:, g, j, :], in_=res[:])
+
+        def n_pass(n, m, groups=range(GROUPS)):
+            if groups[0] == 0:
+                acc["n", n, m] = psum.tile([P, N_TILE], F32, tag="acc", bufs=4, name="acc")
+            cols = slice(n * N_TILE, (n + 1) * N_TILE)
+            rows = slice(m * P, (m + 1) * P)
+            for g in groups:
+                nc.tensor.matmul_mx(
+                    out=acc["n", n, m][:],
+                    lhsT=d_codes[:, g, rows].bitcast(E5M2), lhsT_scale=d_scales[:, g, rows],
+                    rhs=x_codes[:, g, cols].bitcast(E4M3), rhs_scale=x_scales[:, g, cols],
+                    start=(g == 0), stop=(g == GROUPS - 1),
+                )
+
+        out1_v = out_1.rearrange("(m p) w -> p m w", p=P)
+
+        def n_out(n, m):
+            res = work.tile([P, 2, N_TILE], F32, tag="res", bufs=4, name="res")
+            nc.vector.tensor_copy(out=res[:, 0, :], in_=acc["n", n, m][:])
+            nc.scalar.copy(out=res[:, 1, :], in_=acc["n", n, m + 1][:])
+            nc.sync.dma_start(out=out1_v[:, m : m + 2, n * N_TILE : (n + 1) * N_TILE], in_=res[:])
+
+        STEPS = GROUPS * PACK
+
+        def if_slice(s, f, *args):
+            if 0 <= s < STEPS:
+                f(s, *args)
+
+        inter = {"w": w_inter, "x": x_inter, "d": d_inter}
+        quant = {"w": w_quant, "x": x_quant, "d": d_quant}
+
+        def run(s):
+            for task in BG.get(s, "").split():
+                kind, op, i, h = task[:4]
+                if op == "i":
+                    inter[kind](int(i), int(h), task[4])
+                else:
+                    quant[kind](int(i), int(h))
+
+        for s in range(STEPS + 4):
+            if s == 0:
+                front(0)
+                front(1)
+                product(0)
+            run(s)
+            if s == 0:
+                sig(0)
+                sig(1)
+            if_slice(s - 1, turn_out)
+            if s > 0:
+                if_slice(s + 1, sig)
+                if_slice(s + 1, front)
+                if_slice(s, product)
+            if_slice(s - 2, z_quant)
+            if_slice(s, spread)
+            if_slice(s - M_LAG, m_pass)
+            if_slice(s, turn)
+            if_slice(s - M_LAG - 1, m_out, EV[max(0, s - M_LAG - 1) % 12 * 2 : max(0, s - M_LAG - 1) % 12 * 2 + 2])
+            if s == 4:
+                load_group(2)
+                fetch(("g", 2))
+                fetch(("e", 2))
+                fetch(("v", 2), 0, 2)
+                fetch(("v", 2), 2, 4)
+            if s == 5:
+                for g in range(GROUPS):
+                    load(("x", g), xt_v[:, g])
+                    fetch(("x", g))
+        for n in range(2):
+            for m in range(0, 8, 4):
+                if (n, m) in TAIL:
+                    for mm in range(m, m + 4):
+                        n_pass(n, mm, [0, 1])
+                    for mm in range(m, m + 4):
+                        n_pass(n, mm, [2])
+                        if mm % 2:
+                            n_out(n, mm - 1)
+                else:
+                    for mm in range(m, m + 4):
+                        n_pass(n, mm)
+                        if mm % 2:
+                            n_out(n, mm - 1)
+                if n == 0 and m == 0:
+                    run(99)

@@ -8,12 +8,9 @@ P = 128
 PACK = 4
 GROUPS = B // (P * PACK)
 N_TILE = 512
-LOADS = "g0/0/2 w0/0/4 e0/0/2 v0/0/2 w2/0/4 g0/2/4 w1/0/4 w3/0/4 e0/2/4 v0/2/4 g1/0/4 v1/2/4 v1/0/2 e1/0/4"
-GRP = 4
-M_LAG = 3
-EV = "SVSVVSSVVSVSVSVSSSSVSVSS"
-TAIL = {(0, 0), (0, 4), (1, 0)}
-BG = {0:"wi00V wi01S wq00 wi20V wq01",1:"wi21S wi11S wq21 wi31S wq20",2:"wi30V wi10S wq31 wq30 wq11",3:"wq10",5:"di00S",7:"di01S",8:"di10S dq01 dq00",11:"di11S dq10",12:"di20V di21S xi00V dq21 dq20 xq00 dq11",13:"xi10V",14:"xq10 xi20S",15:"xi11S xi21V xi01V xq20 xq21",99:"xq11 xq01"}
+ZC = 6
+TPN = 2
+ORDER = """Lva0/Y Lga0/Y dmu00/V A00/P Lea0/Y sig00/S stt00/V tt00/V Lvb0/Y sig01/S Lgb0/Y Leb0/Y Lvc0/Y stt01/V B00/P dmu01/V a00/S Lgc0/Y tt01/V sig02/S b00/S A01/P B01/P Lec0/Y stt02/V Lw0/Y Lw1/Y dmu02/V a01/S Lw2/Y tt02/V B02/P b01/S Wi01/V Z01/V Wi11/V Wq01/V Wi00/S Wq00/V Wi10/S Wq11/V Wi20/V Wq10/V A02/P Lw3/Y Wi30/V a02/S b02/S Lga1/Y dmu10/V A10/P Wi21/S dmu11/V A11/P Wq30/V Wq20/V Wq21/V Z02/V Wi31/S Lva1/Y a10/S Wq31/V Lvd0/Y Lgd0/Y Z00/V sig10/S Lea1/Y dmu03/V M010/P sig03/S stt10/V M020/P Led0/Y stt03/V M021/P m010/S tt10/V Leb1/Y M000/P a11/S Lgb1/Y dmu13/V M001/P Lvb1/Y m020/S sig11/S m000/S A03/P m001/S B10/P tt03/V a03/S B03/P b10/S Lgb2/Y stt11/V sig12/S dmu12/V Z10/V A13/P a13/S tt11/V b03/S M011/P stt12/V Lga2/Y Lea2/Y sig13/S M101/P Z03/V stt13/V m011/S B11/P dmu20/V m021/S tt13/V A12/P Lva2/Y m101/S tt12/V b11/S dmu22/V Lvb2/Y sig20/S M030/P Leb2/Y M031/P Lx0/Y dmu21/V a12/S Z11/V m030/S B13/P B12/P b13/S A21/P b12/S sig22/S O01/Y dmu23/V A22/P a22/S M100/P Di01/V sig21/S Lx1/Y a21/S Z12/V M120/P m031/S stt20/V m100/S Z13/V Di00/V M121/P sig23/S O00/Y M110/P stt22/V M111/P stt23/V A23/P Di10/S a23/S O02/Y O10/Y A20/P tt20/V a20/S M131/P O03/Y tt22/V B20/P m121/S Lx2/Y B22/P m110/S b20/S stt21/V tt23/V tt21/V b22/S Z22/V M130/P dq01/V Z20/V m120/S B23/P Xi10/S B21/P dq10/V b23/S m131/S m111/S b21/S O11/Y Xi00/V dq00/V M221/P M201/P m201/S M220/P Z23/V O12/Y Xq10/V m220/S m130/S M200/P m200/S M231/P Z21/V m221/S Xq00/V Di20/V M230/P O20/Y Xi20/V Di11/S O22/Y dq20/V m231/S Xq20/V Di21/V O13/Y dq11/V m230/S M211/P O23/Y m211/S N00a/P M210/P m210/S O21/Y N01a/P N00b/P N02a/P N03a/P dq21/V Xi11/V N01b/P n01/V n00/S N02b/P N04a/P N04b/P N05a/P N05b/P Xi01/S Xq11/V Q00/Y N06a/P Xq01/V n02/S Xi21/V Xq21/V N03b/P n03/S Q01/Y n04/S n05/S Q02/Y N06b/P N07a/P N07b/P N14a/P N15a/P N16a/P N17a/P N17b/P n06/S n07/S N15b/P N14b/P n14/S N16b/P n16/S N10a/P N10b/P Q03/Y n15/S n17/V Q17/Y Q14/Y Q16/Y Q15/Y n10/S N11a/P N11b/P n11/S N12a/P N12b/P Q10/Y Q11/Y N13a/P N13b/P n13/V n12/S Q12/Y Q13/Y"""
 FLOPS = 2 * B * D * D * 3
 BYTES = 2 * (3 * B * D + 2 * D * D + B) + 4 * B * D + 4 * (B * D + D * D)
 
@@ -55,168 +52,137 @@ def tile_diffscm_pb_v_kernel(
         d_codes = keep.tile([P, GROUPS, D], U32, align_bytes=64, name="d_codes")
         d_scales = keep.tile([P, GROUPS, D], U8, align_bytes=64, name="d_scales")
 
+        def bf_tile(name):
+            return inp.tile([P, PACK, D], BF16, tag="bf", bufs=8, name=name)
+
         raw = {}
-
-        def load(key, view):
-            tile = inp.tile([P, PACK, D], BF16, tag="bf", bufs=8, name="raw_bf")
-            raw[key] = (tile, view)
-
-        def fetch(key, lo=0, hi=PACK):
-            tile, view = raw[key]
-            nc.sync.dma_start(out=tile[:, lo:hi, :], in_=view[:, lo:hi, :])
-
-        def load_v(g):
-            tile = inp.tile([P, PACK, D], F32, tag="v", bufs=2, name="raw_v")
-            raw["v", g] = (tile, v_v[:, g])
-
-        def load_group(g):
-            load(("g", g), grad_v[:, g])
-            load(("e", g), eps_v[:, g])
-            load_v(g)
-
         for i in range(4):
-            load(("w", i), w_v[i // 2][:, i % 2])
-        load_group(0)
-        load_group(1)
-        nc.scalar.dma_start(out=t_bf[:], in_=t_rand.rearrange("(g p j) o -> p g (j o)", g=GROUPS, j=PACK))
-        for item in LOADS.split():
-            key, lo, hi = item.split("/")
-            fetch((key[0], int(key[1])), int(lo), int(hi))
+            raw["w", i] = bf_tile("raw_bf")
+        for g in range(2):
+            raw["e", g] = bf_tile("raw_bf")
+            raw["g", g] = bf_tile("raw_bf")
+            raw["v", g] = inp.tile([P, PACK, D], F32, tag="v", bufs=2, name="raw_v")
+        views = {"e": eps_v, "g": grad_v, "v": v_v, "x": xt_v}
 
+        nc.scalar.dma_start(out=t_bf[:], in_=t_rand.rearrange("(g p j) o -> p g (j o)", g=GROUPS, j=PACK))
         nc.gpsimd.memset(warm[:], 0.0)
         nc.scalar.activation(out=warm[:], in_=warm[:], func=SIGMOID)
         make_identity(nc, ident[:])
         nc.vector.tensor_copy(out=t_f[:], in_=t_bf[:])
 
-        def interleave(engine, src, half):
-            grp = work.tile([P, N_TILE, PACK], BF16, tag="grp", bufs=GRP, align_bytes=64, name="grp")
-            cols = src[:, :, half * N_TILE : (half + 1) * N_TILE]
-            dst_ap = grp[:].rearrange("p (c i) t -> p c t i", i=4)
-            src_ap = cols.rearrange("p t (c i) -> p c t i", i=4)
+        def copy(engine, out, in_):
             if engine == "V":
-                nc.vector.tensor_copy(out=dst_ap, in_=src_ap)
+                nc.vector.tensor_copy(out=out, in_=in_)
             else:
-                nc.scalar.copy(out=dst_ap, in_=src_ap)
-            return grp
+                nc.scalar.copy(out=out, in_=in_)
 
-        def quantize(grp, codes, scales, fmt):
+        grp, dmu, dv, tps, dzt, dz, acc, res = {}, {}, {}, {}, {}, {}, {}, {}
+
+        def fetch_w(e, i):
+            nc.sync.dma_start(out=raw["w", i][:], in_=w_v[i // 2][:, i % 2])
+
+        def fetch(e, kind, g, lo, hi):
+            if (kind, g) not in raw:
+                if kind == "v":
+                    raw[kind, g] = inp.tile([P, PACK, D], F32, tag="v", bufs=2, name="raw_v")
+                else:
+                    raw[kind, g] = bf_tile("raw_bf")
+            nc.sync.dma_start(out=raw[kind, g][:, lo:hi, :], in_=views[kind][:, g, lo:hi, :])
+
+        def grp_tile(key):
+            if key not in grp:
+                grp[key] = work.tile([P, N_TILE, PACK], BF16, tag="grp", bufs=4, align_bytes=64, name="grp")
+            return grp[key]
+
+        def source(kind, i):
+            return dv[i] if kind == "d" else raw[kind, i]
+
+        def interleave(e, kind, i, h):
+            tile = grp_tile((kind, i, h))
+            cols = source(kind, i)[:, :, h * N_TILE : (h + 1) * N_TILE]
+            copy(e, tile[:].rearrange("p (c i) t -> p c t i", i=4), cols.rearrange("p t (c i) -> p c t i", i=4))
+
+        def quantize(e, kind, i, h):
+            codes, scales, fmt = {"w": (w_codes, w_scales, E4M3), "x": (x_codes, x_scales, E4M3), "d": (d_codes, d_scales, E5M2)}[kind]
+            c = slice(h * N_TILE, (h + 1) * N_TILE)
             nc.vector.quantize_mx(
-                out=codes.bitcast(fmt), scales=scales, in_=grp[:].rearrange("p c t -> p (c t)")
+                out=codes[:, i, c].bitcast(fmt), scales=scales[:, i, c],
+                in_=grp[kind, i, h][:].rearrange("p c t -> p (c t)"),
             )
 
-        pending = {}
-
-        def w_inter(i, h, engine):
-            pending["w", i, h] = interleave(engine, raw["w", i][0], h)
-
-        def w_quant(i, h):
-            c = slice(h * N_TILE, (h + 1) * N_TILE)
-            quantize(pending["w", i, h], w_codes[:, i, c], w_scales[:, i, c], E4M3)
-
-        def x_inter(g, h, engine):
-            pending["x", g, h] = interleave(engine, raw["x", g][0], h)
-
-        def x_quant(g, h):
-            c = slice(h * N_TILE, (h + 1) * N_TILE)
-            quantize(pending["x", g, h], x_codes[:, g, c], x_scales[:, g, c], E4M3)
-
-        dv = {}
-
-        def d_inter(g, h, engine):
-            pending["d", g, h] = interleave(engine, dv[g], h)
-
-        def d_quant(g, h):
-            c = slice(h * N_TILE, (h + 1) * N_TILE)
-            quantize(pending["d", g, h], d_codes[:, g, c], d_scales[:, g, c], E5M2)
-
-        dmu, u, dzt, tps, dz = {}, {}, {}, {}, {}
-
-        def front(s):
-            g, j = divmod(s, PACK)
-            grad = raw["g", g][0][:, j, :]
-            dmu[s] = work.tile([P, D], BF16, tag="dmu", bufs=4, name="dmu")
-            nc.vector.tensor_scalar(out=dmu[s][:], in0=grad, scalar1=t_f[:, g, j : j + 1], scalar2=None, op0=MULT)
-
-        def product(s):
-            g, j = divmod(s, PACK)
-            u[s] = work.tile([P, D], F32, tag="u", bufs=2, name="u")
-            nc.vector.scalar_tensor_tensor(
-                out=u[s][:], in0=raw["g", g][0][:, j, :], scalar=t_f[:, g, j : j + 1],
-                in1=raw["e", g][0][:, j, :], op0=MULT, op1=MULT,
+        def do_dmu(e, g, j):
+            dmu[g, j] = work.tile([P, D], BF16, tag="dmu", bufs=4, name="dmu")
+            nc.vector.tensor_scalar(
+                out=dmu[g, j][:], in0=raw["g", g][:, j, :], scalar1=t_f[:, g, j : j + 1], scalar2=None, op0=MULT
             )
 
-        def sig(s):
-            g, j = divmod(s, PACK)
-            vv = raw["v", g][0][:, j, :]
+        def do_sig(e, g, j):
+            vv = raw["v", g][:, j, :]
             nc.scalar.activation(out=vv, in_=vv, func=SIGMOID)
 
-        def spread(s):
-            g, j = divmod(s, PACK)
-            if j == 0:
+        def do_stt(e, g, j):
+            vv = raw["v", g][:, j, :]
+            nc.vector.scalar_tensor_tensor(
+                out=vv, in0=raw["e", g][:, j, :], scalar=t_f[:, g, j : j + 1], in1=vv, op0=MULT, op1=MULT
+            )
+
+        def do_tt(e, g, j):
+            if g not in dv:
                 dv[g] = work.tile([P, PACK, D], BF16, tag="dv", bufs=2, name="dv")
-            nc.vector.tensor_tensor(out=dv[g][:, j, :], in0=u[s][:], in1=raw["v", g][0][:, j, :], op=MULT)
+            nc.vector.tensor_tensor(out=dv[g][:, j, :], in0=raw["v", g][:, j, :], in1=raw["g", g][:, j, :], op=MULT)
 
-        def turn(s):
-            g, j = divmod(s, PACK)
-            for head, src in ((0, dmu[s][:]), (1, dv[g][:, j, :])):
-                words = src.bitcast(F32)
-                tp = psum.tile([P, 2, 2, P], F32, tag="tp", bufs=4, name="tp")
-                for k in range(2):
-                    for w in range(2):
-                        nc.tensor.transpose(tp[:, k, w, :], words[:, 256 * k + w : 256 * (k + 1) : 2], ident[:])
-                tps[s, head] = tp
+        def turn(e, g, j, head):
+            words = (dv[g][:, j, :] if head else dmu[g, j][:]).bitcast(F32)
+            tp = psum.tile([P, 2, 2, P], F32, tag="tp", bufs=TPN, name="tp")
+            for k in range(2):
+                for w in range(2):
+                    nc.tensor.transpose(tp[:, k, w, :], words[:, 256 * k + w : 256 * (k + 1) : 2], ident[:])
+            tps[g, j, head] = tp
 
-        def turn_out(s):
-            dzt[s] = work.tile([P, 2, 2, P, PACK], BF16, tag="dzt", bufs=3, align_bytes=64, name="dzt")
-            for head in range(2):
-                dst = dzt[s][:, head].rearrange("p k c t -> p (k c t)").bitcast(F32)
-                nc.scalar.copy(
-                    out=dst.rearrange("p (k c w) -> p k c w", k=2, w=2),
-                    in_=tps[s, head][:].rearrange("p k w c -> p k c w"),
+        def turn_out(e, g, j, head):
+            if (g, j) not in dzt:
+                dzt[g, j] = work.tile([P, 2, 2, P, PACK], BF16, tag="dzt", bufs=4, align_bytes=64, name="dzt")
+            dst = dzt[g, j][:, head].rearrange("p k c t -> p (k c t)").bitcast(F32)
+            copy(e, dst.rearrange("p (k c w) -> p k c w", k=2, w=2), tps[g, j, head][:].rearrange("p k w c -> p k c w"))
+
+        def z_quant(e, g, j):
+            codes = work.tile([P, 4 * P], U32, tag="zc", bufs=ZC, align_bytes=64, name="zc")
+            scales = work.tile([P, 4 * P], U8, tag="zs", bufs=ZC, align_bytes=64, name="zs")
+            nc.vector.quantize_mx(
+                out=codes[:].bitcast(E5M2), scales=scales[:], in_=dzt[g, j][:].rearrange("p h k c t -> p (h k c t)")
+            )
+            dz[g, j] = (codes, scales)
+
+        def m_pass(e, g, j, n):
+            acc[g, j, n] = psum.tile([P, N_TILE], F32, tag="acc", bufs=8 - TPN, name="acc")
+            cols = slice(n * N_TILE, (n + 1) * N_TILE)
+            for i in range(4):
+                codes, scales = dz[g, j]
+                rows = slice(i * P, (i + 1) * P)
+                nc.tensor.matmul_mx(
+                    out=acc[g, j, n][:],
+                    lhsT=codes[:, rows].bitcast(E5M2), lhsT_scale=scales[:, rows],
+                    rhs=w_codes[:, i, cols].bitcast(E4M3), rhs_scale=w_scales[:, i, cols],
+                    start=(i == 0), stop=(i == 3),
                 )
 
-        def z_quant(s):
-            codes = work.tile([P, 4 * P], U32, tag="zc", bufs=4, align_bytes=64, name="zc")
-            scales = work.tile([P, 4 * P], U8, tag="zs", bufs=4, align_bytes=64, name="zs")
-            nc.vector.quantize_mx(
-                out=codes[:].bitcast(E5M2), scales=scales[:],
-                in_=dzt[s][:].rearrange("p h k c t -> p (h k c t)"),
-            )
-            dz[s] = (codes, scales)
+        def res_tile(key):
+            if key not in res:
+                res[key] = work.tile([P, 2, N_TILE], F32, tag="res", bufs=5, name="res")
+            return res[key]
 
-        acc = {}
+        def m_out(e, g, j, n):
+            copy(e, res_tile((g, j))[:, n, :], acc[g, j, n][:])
 
-        def m_pass(s):
-            codes, scales = dz[s]
-            for n in range(2):
-                acc[s, n] = psum.tile([P, N_TILE], F32, tag="acc", bufs=4, name="acc")
-                cols = slice(n * N_TILE, (n + 1) * N_TILE)
-                for i in range(4):
-                    rows = slice(i * P, (i + 1) * P)
-                    nc.tensor.matmul_mx(
-                        out=acc[s, n][:],
-                        lhsT=codes[:, rows].bitcast(E5M2), lhsT_scale=scales[:, rows],
-                        rhs=w_codes[:, i, cols].bitcast(E4M3), rhs_scale=w_scales[:, i, cols],
-                        start=(i == 0), stop=(i == 3),
-                    )
+        def m_store(e, g, j):
+            nc.sync.dma_start(out=out0_v[:, g, j, :], in_=res[g, j][:].rearrange("p n w -> p (n w)"))
 
-        def m_out(s, engines):
-            g, j = divmod(s, PACK)
-            res = work.tile([P, D], F32, tag="res", bufs=4, name="res")
-            for n in range(2):
-                dst = res[:, n * N_TILE : (n + 1) * N_TILE]
-                if engines[n] == "V":
-                    nc.vector.tensor_copy(out=dst, in_=acc[s, n][:])
-                else:
-                    nc.scalar.copy(out=dst, in_=acc[s, n][:])
-            nc.sync.dma_start(out=out0_v[:, g, j, :], in_=res[:])
-
-        def n_pass(n, m, groups=range(GROUPS)):
-            if groups[0] == 0:
-                acc["n", n, m] = psum.tile([P, N_TILE], F32, tag="acc", bufs=4, name="acc")
+        def n_pass(e, n, m, part):
+            if part == "a":
+                acc["n", n, m] = psum.tile([P, N_TILE], F32, tag="acc", bufs=8 - TPN, name="acc")
             cols = slice(n * N_TILE, (n + 1) * N_TILE)
             rows = slice(m * P, (m + 1) * P)
-            for g in groups:
+            for g in ([0, 1] if part == "a" else [2]):
                 nc.tensor.matmul_mx(
                     out=acc["n", n, m][:],
                     lhsT=d_codes[:, g, rows].bitcast(E5M2), lhsT_scale=d_scales[:, g, rows],
@@ -226,71 +192,59 @@ def tile_diffscm_pb_v_kernel(
 
         out1_v = out_1.rearrange("(m p) w -> p m w", p=P)
 
-        def n_out(n, m):
-            res = work.tile([P, 2, N_TILE], F32, tag="res", bufs=4, name="res")
-            nc.vector.tensor_copy(out=res[:, 0, :], in_=acc["n", n, m][:])
-            nc.scalar.copy(out=res[:, 1, :], in_=acc["n", n, m + 1][:])
-            nc.sync.dma_start(out=out1_v[:, m : m + 2, n * N_TILE : (n + 1) * N_TILE], in_=res[:])
+        def n_out(e, n, m):
+            copy(e, res_tile(("n", n, m // 2))[:, m % 2, :], acc["n", n, m][:])
 
-        STEPS = GROUPS * PACK
+        def n_store(e, n, q):
+            cols = slice(n * N_TILE, (n + 1) * N_TILE)
+            if n == 0:
+                nc.sync.dma_start(out=out1_v[:, 2 * q : 2 * q + 2, cols], in_=res["n", n, q][:])
+            else:
+                nc.sync.dma_start(out=out1_v[:, q, cols], in_=res["n", n, q // 2][:, q % 2, :])
 
-        def if_slice(s, f, *args):
-            if 0 <= s < STEPS:
-                f(s, *args)
-
-        inter = {"w": w_inter, "x": x_inter, "d": d_inter}
-        quant = {"w": w_quant, "x": x_quant, "d": d_quant}
-
-        def run(s):
-            for task in BG.get(s, "").split():
-                kind, op, i, h = task[:4]
-                if op == "i":
-                    inter[kind](int(i), int(h), task[4])
+        kinds = {"W": "w", "D": "d", "X": "x"}
+        for item in ORDER.split():
+            name, e = item.split("/")
+            d = [int(ch) for ch in name if ch in "0123456789"]
+            c = name[0]
+            if c == "L":
+                if name[1] == "w":
+                    fetch_w(e, d[0])
+                elif name[1] == "x":
+                    fetch(e, "x", d[0], 0, PACK)
                 else:
-                    quant[kind](int(i), int(h))
-
-        for s in range(STEPS + 4):
-            if s == 0:
-                front(0)
-                front(1)
-                product(0)
-            run(s)
-            if s == 0:
-                sig(0)
-                sig(1)
-            if_slice(s - 1, turn_out)
-            if s > 0:
-                if_slice(s + 1, sig)
-                if_slice(s + 1, front)
-                if_slice(s, product)
-            if_slice(s - 2, z_quant)
-            if_slice(s, spread)
-            if_slice(s - M_LAG, m_pass)
-            if_slice(s, turn)
-            if_slice(s - M_LAG - 1, m_out, EV[max(0, s - M_LAG - 1) % 12 * 2 : max(0, s - M_LAG - 1) % 12 * 2 + 2])
-            if s == 4:
-                load_group(2)
-                fetch(("g", 2))
-                fetch(("e", 2))
-                fetch(("v", 2), 0, 2)
-                fetch(("v", 2), 2, 4)
-            if s == 5:
-                for g in range(GROUPS):
-                    load(("x", g), xt_v[:, g])
-                    fetch(("x", g))
-        for n in range(2):
-            for m in range(0, 8, 4):
-                if (n, m) in TAIL:
-                    for mm in range(m, m + 4):
-                        n_pass(n, mm, [0, 1])
-                    for mm in range(m, m + 4):
-                        n_pass(n, mm, [2])
-                        if mm % 2:
-                            n_out(n, mm - 1)
+                    step = 1 if d[0] == 0 else 2
+                    lo = ["a", "b", "c", "d"].index(name[2]) * step
+                    fetch(e, name[1], d[0], lo, lo + step)
+            elif c in kinds or name[:2] == "dq":
+                kind = kinds.get(c, "d")
+                if name[1] == "q":
+                    quantize(e, kind, d[0], d[1])
                 else:
-                    for mm in range(m, m + 4):
-                        n_pass(n, mm)
-                        if mm % 2:
-                            n_out(n, mm - 1)
-                if n == 0 and m == 0:
-                    run(99)
+                    interleave(e, kind, d[0], d[1])
+            elif name.startswith("dmu"):
+                do_dmu(e, d[0], d[1])
+            elif name.startswith("sig"):
+                do_sig(e, d[0], d[1])
+            elif name.startswith("stt"):
+                do_stt(e, d[0], d[1])
+            elif name.startswith("tt"):
+                do_tt(e, d[0], d[1])
+            elif c in "AB":
+                turn(e, d[0], d[1], int(c == "B"))
+            elif c in "ab":
+                turn_out(e, d[0], d[1], int(c == "b"))
+            elif c == "Z":
+                z_quant(e, d[0], d[1])
+            elif c == "M":
+                m_pass(e, d[0], d[1], d[2])
+            elif c == "m":
+                m_out(e, d[0], d[1], d[2])
+            elif c == "O":
+                m_store(e, d[0], d[1])
+            elif c == "N":
+                n_pass(e, d[0], d[1], name[3])
+            elif c == "n":
+                n_out(e, d[0], d[1])
+            else:
+                n_store(e, d[0], d[1])

from contextlib import ExitStack

import concourse.mybir as mybir
from concourse.masks import make_identity

B, D = 1536, 1024
P = 128
PACK = 4
GROUPS = B // (P * PACK)
N_TILE = 512
ZC = 6
TPN = 2
ORDER = """Lva0/Y Lga0/Y dmu00/V A00/P Lea0/Y sig00/S stt00/V tt00/V Lvb0/Y sig01/S Lgb0/Y Leb0/Y Lvc0/Y stt01/V B00/P dmu01/V a00/S Lgc0/Y tt01/V sig02/S b00/S A01/P B01/P Lec0/Y stt02/V Lw0/Y Lw1/Y dmu02/V a01/S Lw2/Y tt02/V B02/P b01/S Wi01/V Z01/V Wi11/V Wq01/V Wi00/S Wq00/V Wi10/S Wq11/V Wi20/V Wq10/V A02/P Lw3/Y Wi30/V a02/S b02/S Lga1/Y dmu10/V A10/P Wi21/S dmu11/V A11/P Wq30/V Wq20/V Wq21/V Z02/V Wi31/S Lva1/Y a10/S Wq31/V Lvd0/Y Lgd0/Y Z00/V sig10/S Lea1/Y dmu03/V M010/P sig03/S stt10/V M020/P Led0/Y stt03/V M021/P m010/S tt10/V Leb1/Y M000/P a11/S Lgb1/Y dmu13/V M001/P Lvb1/Y m020/S sig11/S m000/S A03/P m001/S B10/P tt03/V a03/S B03/P b10/S Lgb2/Y stt11/V sig12/S dmu12/V Z10/V A13/P a13/S tt11/V b03/S M011/P stt12/V Lga2/Y Lea2/Y sig13/S M101/P Z03/V stt13/V m011/S B11/P dmu20/V m021/S tt13/V A12/P Lva2/Y m101/S tt12/V b11/S dmu22/V Lvb2/Y sig20/S M030/P Leb2/Y M031/P Lx0/Y dmu21/V a12/S Z11/V m030/S B13/P B12/P b13/S A21/P b12/S sig22/S O01/Y dmu23/V A22/P a22/S M100/P Di01/V sig21/S Lx1/Y a21/S Z12/V M120/P m031/S stt20/V m100/S Z13/V Di00/V M121/P sig23/S O00/Y M110/P stt22/V M111/P stt23/V A23/P Di10/S a23/S O02/Y O10/Y A20/P tt20/V a20/S M131/P O03/Y tt22/V B20/P m121/S Lx2/Y B22/P m110/S b20/S stt21/V tt23/V tt21/V b22/S Z22/V M130/P dq01/V Z20/V m120/S B23/P Xi10/S B21/P dq10/V b23/S m131/S m111/S b21/S O11/Y Xi00/V dq00/V M221/P M201/P m201/S M220/P Z23/V O12/Y Xq10/V m220/S m130/S M200/P m200/S M231/P Z21/V m221/S Xq00/V Di20/V M230/P O20/Y Xi20/V Di11/S O22/Y dq20/V m231/S Xq20/V Di21/V O13/Y dq11/V m230/S M211/P O23/Y m211/S N00a/P M210/P m210/S O21/Y N01a/P N00b/P N02a/P N03a/P dq21/V Xi11/V N01b/P n01/V n00/S N02b/P N04a/P N04b/P N05a/P N05b/P Xi01/S Xq11/V Q00/Y N06a/P Xq01/V n02/S Xi21/V Xq21/V N03b/P n03/S Q01/Y n04/S n05/S Q02/Y N06b/P N07a/P N07b/P N14a/P N15a/P N16a/P N17a/P N17b/P n06/S n07/S N15b/P N14b/P n14/S N16b/P n16/S N10a/P N10b/P Q03/Y n15/S n17/V Q17/Y Q14/Y Q16/Y Q15/Y n10/S N11a/P N11b/P n11/S N12a/P N12b/P Q10/Y Q11/Y N13a/P N13b/P n13/V n12/S Q12/Y Q13/Y"""
FLOPS = 2 * B * D * D * 3
BYTES = 2 * (3 * B * D + 2 * D * D + B) + 4 * B * D + 4 * (B * D + D * D)

F32 = mybir.dt.float32
BF16 = mybir.dt.bfloat16
U32 = mybir.dt.uint32
U8 = mybir.dt.uint8
E4M3 = mybir.dt.float8_e4m3fn_x4
E5M2 = mybir.dt.float8_e5m2_x4
MULT = mybir.AluOpType.mult
SIGMOID = mybir.ActivationFunctionType.Sigmoid


def tile_diffscm_pb_v_kernel(
    tc, xt, eps, x, t_rand, Wm, bm, Wv, bv, v, grad_out, out_0, out_1
):
    nc = tc.nc
    by_group = lambda a: a.rearrange("(g p j) w -> p g j w", g=GROUPS, j=PACK)
    xt_v, eps_v, v_v, grad_v, out0_v = [by_group(a) for a in (xt, eps, v, grad_out, out_0)]
    w_v = [w.rearrange("(g p j) w -> p g j w", g=2, j=PACK) for w in (Wm, Wv)]

    with ExitStack() as ctx:
        const = ctx.enter_context(tc.tile_pool(name="const", bufs=1))
        inp = ctx.enter_context(tc.tile_pool(name="inp", bufs=1))
        keep = ctx.enter_context(tc.tile_pool(name="keep", bufs=1))
        work = ctx.enter_context(tc.tile_pool(name="work", bufs=1))
        psum = ctx.enter_context(tc.psum_pool(name="psum", bufs=4))
        ctx.enter_context(tc.manual_schedule())

        t_bf = const.tile([P, GROUPS, PACK], BF16, name="t_bf")
        t_f = const.tile([P, GROUPS, PACK], F32, name="t_f")
        warm = const.tile([P, 1], F32, name="warm")
        ident = const.tile([P, P], F32, name="ident")

        w_codes = keep.tile([P, 4, D], U32, align_bytes=64, name="w_codes")
        w_scales = keep.tile([P, 4, D], U8, align_bytes=64, name="w_scales")
        x_codes = keep.tile([P, GROUPS, D], U32, align_bytes=64, name="x_codes")
        x_scales = keep.tile([P, GROUPS, D], U8, align_bytes=64, name="x_scales")
        d_codes = keep.tile([P, GROUPS, D], U32, align_bytes=64, name="d_codes")
        d_scales = keep.tile([P, GROUPS, D], U8, align_bytes=64, name="d_scales")

        def bf_tile(name):
            return inp.tile([P, PACK, D], BF16, tag="bf", bufs=8, name=name)

        raw = {}
        for i in range(4):
            raw["w", i] = bf_tile("raw_bf")
        for g in range(2):
            raw["e", g] = bf_tile("raw_bf")
            raw["g", g] = bf_tile("raw_bf")
            raw["v", g] = inp.tile([P, PACK, D], F32, tag="v", bufs=2, name="raw_v")
        views = {"e": eps_v, "g": grad_v, "v": v_v, "x": xt_v}

        nc.scalar.dma_start(out=t_bf[:], in_=t_rand.rearrange("(g p j) o -> p g (j o)", g=GROUPS, j=PACK))
        nc.gpsimd.memset(warm[:], 0.0)
        nc.scalar.activation(out=warm[:], in_=warm[:], func=SIGMOID)
        make_identity(nc, ident[:])
        nc.vector.tensor_copy(out=t_f[:], in_=t_bf[:])

        def copy(engine, out, in_):
            if engine == "V":
                nc.vector.tensor_copy(out=out, in_=in_)
            else:
                nc.scalar.copy(out=out, in_=in_)

        grp, dmu, dv, tps, dzt, dz, acc, res = {}, {}, {}, {}, {}, {}, {}, {}

        def fetch_w(e, i):
            nc.sync.dma_start(out=raw["w", i][:], in_=w_v[i // 2][:, i % 2])

        def fetch(e, kind, g, lo, hi):
            if (kind, g) not in raw:
                if kind == "v":
                    raw[kind, g] = inp.tile([P, PACK, D], F32, tag="v", bufs=2, name="raw_v")
                else:
                    raw[kind, g] = bf_tile("raw_bf")
            nc.sync.dma_start(out=raw[kind, g][:, lo:hi, :], in_=views[kind][:, g, lo:hi, :])

        def grp_tile(key):
            if key not in grp:
                grp[key] = work.tile([P, N_TILE, PACK], BF16, tag="grp", bufs=4, align_bytes=64, name="grp")
            return grp[key]

        def source(kind, i):
            return dv[i] if kind == "d" else raw[kind, i]

        def interleave(e, kind, i, h):
            tile = grp_tile((kind, i, h))
            cols = source(kind, i)[:, :, h * N_TILE : (h + 1) * N_TILE]
            copy(e, tile[:].rearrange("p (c i) t -> p c t i", i=4), cols.rearrange("p t (c i) -> p c t i", i=4))

        def quantize(e, kind, i, h):
            codes, scales, fmt = {"w": (w_codes, w_scales, E4M3), "x": (x_codes, x_scales, E4M3), "d": (d_codes, d_scales, E5M2)}[kind]
            c = slice(h * N_TILE, (h + 1) * N_TILE)
            nc.vector.quantize_mx(
                out=codes[:, i, c].bitcast(fmt), scales=scales[:, i, c],
                in_=grp[kind, i, h][:].rearrange("p c t -> p (c t)"),
            )

        def do_dmu(e, g, j):
            dmu[g, j] = work.tile([P, D], BF16, tag="dmu", bufs=4, name="dmu")
            nc.vector.tensor_scalar(
                out=dmu[g, j][:], in0=raw["g", g][:, j, :], scalar1=t_f[:, g, j : j + 1], scalar2=None, op0=MULT
            )

        def do_sig(e, g, j):
            vv = raw["v", g][:, j, :]
            nc.scalar.activation(out=vv, in_=vv, func=SIGMOID)

        def do_stt(e, g, j):
            vv = raw["v", g][:, j, :]
            nc.vector.scalar_tensor_tensor(
                out=vv, in0=raw["e", g][:, j, :], scalar=t_f[:, g, j : j + 1], in1=vv, op0=MULT, op1=MULT
            )

        def do_tt(e, g, j):
            if g not in dv:
                dv[g] = work.tile([P, PACK, D], BF16, tag="dv", bufs=2, name="dv")
            nc.vector.tensor_tensor(out=dv[g][:, j, :], in0=raw["v", g][:, j, :], in1=raw["g", g][:, j, :], op=MULT)

        def turn(e, g, j, head):
            words = (dv[g][:, j, :] if head else dmu[g, j][:]).bitcast(F32)
            tp = psum.tile([P, 2, 2, P], F32, tag="tp", bufs=TPN, name="tp")
            for k in range(2):
                for w in range(2):
                    nc.tensor.transpose(tp[:, k, w, :], words[:, 256 * k + w : 256 * (k + 1) : 2], ident[:])
            tps[g, j, head] = tp

        def turn_out(e, g, j, head):
            if (g, j) not in dzt:
                dzt[g, j] = work.tile([P, 2, 2, P, PACK], BF16, tag="dzt", bufs=4, align_bytes=64, name="dzt")
            dst = dzt[g, j][:, head].rearrange("p k c t -> p (k c t)").bitcast(F32)
            copy(e, dst.rearrange("p (k c w) -> p k c w", k=2, w=2), tps[g, j, head][:].rearrange("p k w c -> p k c w"))

        def z_quant(e, g, j):
            codes = work.tile([P, 4 * P], U32, tag="zc", bufs=ZC, align_bytes=64, name="zc")
            scales = work.tile([P, 4 * P], U8, tag="zs", bufs=ZC, align_bytes=64, name="zs")
            nc.vector.quantize_mx(
                out=codes[:].bitcast(E5M2), scales=scales[:], in_=dzt[g, j][:].rearrange("p h k c t -> p (h k c t)")
            )
            dz[g, j] = (codes, scales)

        def m_pass(e, g, j, n):
            acc[g, j, n] = psum.tile([P, N_TILE], F32, tag="acc", bufs=8 - TPN, name="acc")
            cols = slice(n * N_TILE, (n + 1) * N_TILE)
            for i in range(4):
                codes, scales = dz[g, j]
                rows = slice(i * P, (i + 1) * P)
                nc.tensor.matmul_mx(
                    out=acc[g, j, n][:],
                    lhsT=codes[:, rows].bitcast(E5M2), lhsT_scale=scales[:, rows],
                    rhs=w_codes[:, i, cols].bitcast(E4M3), rhs_scale=w_scales[:, i, cols],
                    start=(i == 0), stop=(i == 3),
                )

        def res_tile(key):
            if key not in res:
                res[key] = work.tile([P, 2, N_TILE], F32, tag="res", bufs=5, name="res")
            return res[key]

        def m_out(e, g, j, n):
            copy(e, res_tile((g, j))[:, n, :], acc[g, j, n][:])

        def m_store(e, g, j):
            nc.sync.dma_start(out=out0_v[:, g, j, :], in_=res[g, j][:].rearrange("p n w -> p (n w)"))

        def n_pass(e, n, m, part):
            if part == "a":
                acc["n", n, m] = psum.tile([P, N_TILE], F32, tag="acc", bufs=8 - TPN, name="acc")
            cols = slice(n * N_TILE, (n + 1) * N_TILE)
            rows = slice(m * P, (m + 1) * P)
            for g in ([0, 1] if part == "a" else [2]):
                nc.tensor.matmul_mx(
                    out=acc["n", n, m][:],
                    lhsT=d_codes[:, g, rows].bitcast(E5M2), lhsT_scale=d_scales[:, g, rows],
                    rhs=x_codes[:, g, cols].bitcast(E4M3), rhs_scale=x_scales[:, g, cols],
                    start=(g == 0), stop=(g == GROUPS - 1),
                )

        out1_v = out_1.rearrange("(m p) w -> p m w", p=P)

        def n_out(e, n, m):
            copy(e, res_tile(("n", n, m // 2))[:, m % 2, :], acc["n", n, m][:])

        def n_store(e, n, q):
            cols = slice(n * N_TILE, (n + 1) * N_TILE)
            if n == 0:
                nc.sync.dma_start(out=out1_v[:, 2 * q : 2 * q + 2, cols], in_=res["n", n, q][:])
            else:
                nc.sync.dma_start(out=out1_v[:, q, cols], in_=res["n", n, q // 2][:, q % 2, :])

        kinds = {"W": "w", "D": "d", "X": "x"}
        for item in ORDER.split():
            name, e = item.split("/")
            d = [int(ch) for ch in name if ch in "0123456789"]
            c = name[0]
            if c == "L":
                if name[1] == "w":
                    fetch_w(e, d[0])
                elif name[1] == "x":
                    fetch(e, "x", d[0], 0, PACK)
                else:
                    step = 1 if d[0] == 0 else 2
                    lo = ["a", "b", "c", "d"].index(name[2]) * step
                    fetch(e, name[1], d[0], lo, lo + step)
            elif c in kinds or name[:2] == "dq":
                kind = kinds.get(c, "d")
                if name[1] == "q":
                    quantize(e, kind, d[0], d[1])
                else:
                    interleave(e, kind, d[0], d[1])
            elif name.startswith("dmu"):
                do_dmu(e, d[0], d[1])
            elif name.startswith("sig"):
                do_sig(e, d[0], d[1])
            elif name.startswith("stt"):
                do_stt(e, d[0], d[1])
            elif name.startswith("tt"):
                do_tt(e, d[0], d[1])
            elif c in "AB":
                turn(e, d[0], d[1], int(c == "B"))
            elif c in "ab":
                turn_out(e, d[0], d[1], int(c == "b"))
            elif c == "Z":
                z_quant(e, d[0], d[1])
            elif c == "M":
                m_pass(e, d[0], d[1], d[2])
            elif c == "m":
                m_out(e, d[0], d[1], d[2])
            elif c == "O":
                m_store(e, d[0], d[1])
            elif c == "N":
                n_pass(e, d[0], d[1], name[3])
            elif c == "n":
                n_out(e, d[0], d[1])
            else:
                n_store(e, d[0], d[1])
